import numpy as np
import ml_dtypes

BF16 = ml_dtypes.bfloat16


def bf(x):
    return np.asarray(x, np.float32).astype(BF16)


def f32(x):
    return np.asarray(x, np.float32)


def f64(x):
    return np.asarray(x).astype(np.float64)


def striped(idx):
    return np.tile(idx.reshape(-1, 16).T, (8, 1))


H, T, S, N, R = 2, 128, 256, 192, 256


def setup_inputs():
    return {"base": f32(np.random.standard_normal((R, S))), "fresh": f32(np.random.standard_normal((R, N))), "offs": striped(np.random.permutation(S)[:N])}


def reference(base, fresh, offs):
    idx = offs[:16].T.reshape(-1)
    logit = f64(base).copy()
    logit[:, idx] = f64(fresh)
    e = np.exp(logit)
    own = np.tile(np.arange(T) + 1.0, H)[:, None]
    return S * e / (e.sum(axis=1, keepdims=True) + own)

@@ -1,0 +1,56 @@
+import concourse.mybir as mybir
+
+F32 = mybir.dt.float32
+U16 = mybir.dt.uint16
+ACT = mybir.ActivationFunctionType
+ALU = mybir.AluOpType
+AXIS = mybir.AxisListType
+
+P = 128
+HEADS = 2
+SLOTS = 256
+N = 192
+
+
+def tile_causalselfattention_kernel(tc, base, fresh, offs, out):
+    nc = tc.nc
+    with (
+        tc.tile_pool(name="held", bufs=1) as held,
+        tc.tile_pool(name="work", bufs=HEADS) as work,
+    ):
+        offsets = held.tile([P, N // 16], U16, name="offsets")
+        nc.sync.dma_start(offsets[:], offs)
+
+        self_keys = held.tile([P, 1], F32, name="self_keys")
+        nc.gpsimd.iota(
+            self_keys[:], pattern=[[0, 1]], base=1, channel_multiplier=1, allow_small_or_imprecise_dtypes=True
+        )
+
+        for head in range(HEADS):
+            rows = slice(head * P, (head + 1) * P)
+            logits = work.tile([P, SLOTS], F32, name="logits")
+            nc.sync.dma_start(logits[:], base[rows, :])
+            retrieved = work.tile([P, N], F32, name="retrieved")
+            nc.scalar.dma_start(retrieved[:], fresh[rows, :])
+
+            nc.scalar.activation(logits[:].indirect(offsets[:]), retrieved[:], ACT.Copy)
+
+            shift = work.tile([P, 1], F32, name="shift")
+            nc.vector.reduce_max(shift[:], logits[:], axis=AXIS.X, negate=True)
+            nc.vector.tensor_scalar_min(shift[:], shift[:], 0.0)
+
+            self_weight = work.tile([P, 1], F32, name="self_weight")
+            nc.scalar.activation(self_weight[:], shift[:], ACT.Exp)
+            weights = work.tile([P, SLOTS], F32, name="weights")
+            slot_sum = work.tile([P, 1], F32, name="slot_sum")
+            nc.scalar.activation(weights[:], logits[:], ACT.Exp, bias=shift[:], accum_out=slot_sum[:])
+
+            denominator = work.tile([P, 1], F32, name="denominator")
+            nc.vector.scalar_tensor_tensor(
+                denominator[:], self_weight[:], self_keys[:], slot_sum[:], op0=ALU.mult, op1=ALU.add
+            )
+            inverse = work.tile([P, 1], F32, name="inverse")
+            nc.vector.reciprocal(inverse[:], denominator[:])
+
+            nc.vector.tensor_scalar(weights[:], weights[:], inverse[:], float(SLOTS), op0=ALU.mult, op1=ALU.mult)
+            nc.sync.dma_start(out[rows, :], weights[:])

@@ -26,12 +26,25 @@ def tile_causalselfattention_kernel(tc, base, fresh, offs, out):
             self_keys[:], pattern=[[0, 1]], base=1, channel_multiplier=1, allow_small_or_imprecise_dtypes=True
         )
 
+        logits_of = []
+        retrieved_of = []
         for head in range(HEADS):
             rows = slice(head * P, (head + 1) * P)
             logits = work.tile([P, SLOTS], F32, name="logits")
             nc.sync.dma_start(logits[:], base[rows, :])
             retrieved = work.tile([P, N], F32, name="retrieved")
             nc.scalar.dma_start(retrieved[:], fresh[rows, :])
+            logits_of.append(logits)
+            retrieved_of.append(retrieved)
+
+        warm = held.tile([P, 1], F32, name="warm")
+        nc.vector.memset(warm[:], 0.0)
+        nc.scalar.activation(warm[:], warm[:], ACT.Exp)
+
+        for head in range(HEADS):
+            rows = slice(head * P, (head + 1) * P)
+            logits = logits_of[head]
+            retrieved = retrieved_of[head]
 
             nc.scalar.activation(logits[:].indirect(offsets[:]), retrieved[:], ACT.Copy)
 

@@ -4,7 +4,6 @@ F32 = mybir.dt.float32
 U16 = mybir.dt.uint16
 ACT = mybir.ActivationFunctionType
 ALU = mybir.AluOpType
-AXIS = mybir.AxisListType
 
 P = 128
 HEADS = 2
@@ -48,15 +47,15 @@ def tile_causalselfattention_kernel(tc, base, fresh, offs, out):
 
             nc.scalar.activation(logits[:].indirect(offsets[:]), retrieved[:], ACT.Copy)
 
+            negated = work.tile([P, SLOTS], F32, name="negated")
             shift = work.tile([P, 1], F32, name="shift")
-            nc.vector.reduce_max(shift[:], logits[:], axis=AXIS.X, negate=True)
-            nc.vector.tensor_scalar_min(shift[:], shift[:], 0.0)
+            nc.vector.tensor_scalar(negated[:], logits[:], -1.0, 0.0, op0=ALU.mult, op1=ALU.min, accum_out=shift[:])
 
             self_weight = work.tile([P, 1], F32, name="self_weight")
             nc.scalar.activation(self_weight[:], shift[:], ACT.Exp)
             weights = work.tile([P, SLOTS], F32, name="weights")
             slot_sum = work.tile([P, 1], F32, name="slot_sum")
-            nc.scalar.activation(weights[:], logits[:], ACT.Exp, bias=shift[:], accum_out=slot_sum[:])
+            nc.scalar.activation(weights[:], negated[:], ACT.Exp, bias=shift[:], scale=-1.0, accum_out=slot_sum[:])
 
             denominator = work.tile([P, 1], F32, name="denominator")
             nc.vector.scalar_tensor_tensor(

@@ -9,6 +9,8 @@ P = 128
 HEADS = 2
 SLOTS = 256
 N = 192
+KEYS = SLOTS + P
+MASKED = 1.0e4
 
 
 def tile_causalselfattention_kernel(tc, base, fresh, offs, out):
@@ -19,11 +21,6 @@ def tile_causalselfattention_kernel(tc, base, fresh, offs, out):
     ):
         offsets = held.tile([P, N // 16], U16, name="offsets")
         nc.sync.dma_start(offsets[:], offs)
-
-        self_keys = held.tile([P, 1], F32, name="self_keys")
-        nc.gpsimd.iota(
-            self_keys[:], pattern=[[0, 1]], base=1, channel_multiplier=1, allow_small_or_imprecise_dtypes=True
-        )
 
         logits_of = []
         retrieved_of = []
@@ -40,29 +37,38 @@ def tile_causalselfattention_kernel(tc, base, fresh, offs, out):
         nc.vector.memset(warm[:], 0.0)
         nc.scalar.activation(warm[:], warm[:], ACT.Exp)
 
+        causal = held.tile([P, P], F32, name="causal")
+        nc.gpsimd.memset(causal[:], 0.0)
+        nc.gpsimd.affine_select(
+            causal[:], causal[:], pattern=[[-1, P]], compare_op=ALU.is_ge, fill=MASKED, base=0, channel_multiplier=1
+        )
+        negated_of = []
+        for head in range(HEADS):
+            negated = work.tile([P, KEYS], F32, name="negated")
+            nc.gpsimd.tensor_copy(negated[:, SLOTS:KEYS], causal[:])
+            negated_of.append(negated)
+
         for head in range(HEADS):
             rows = slice(head * P, (head + 1) * P)
             logits = logits_of[head]
-            retrieved = retrieved_of[head]
+            negated = negated_of[head]
 
-            nc.scalar.activation(logits[:].indirect(offsets[:]), retrieved[:], ACT.Copy)
+            nc.scalar.activation(logits[:].indirect(offsets[:]), retrieved_of[head][:], ACT.Copy)
 
-            negated = work.tile([P, SLOTS], F32, name="negated")
             shift = work.tile([P, 1], F32, name="shift")
-            nc.vector.tensor_scalar(negated[:], logits[:], -1.0, 0.0, op0=ALU.mult, op1=ALU.min, accum_out=shift[:])
-
-            self_weight = work.tile([P, 1], F32, name="self_weight")
-            nc.scalar.activation(self_weight[:], shift[:], ACT.Exp)
-            weights = work.tile([P, SLOTS], F32, name="weights")
-            slot_sum = work.tile([P, 1], F32, name="slot_sum")
-            nc.scalar.activation(weights[:], negated[:], ACT.Exp, bias=shift[:], scale=-1.0, accum_out=slot_sum[:])
-
-            denominator = work.tile([P, 1], F32, name="denominator")
-            nc.vector.scalar_tensor_tensor(
-                denominator[:], self_weight[:], self_keys[:], slot_sum[:], op0=ALU.mult, op1=ALU.add
+            nc.vector.tensor_scalar(
+                negated[:, 0:SLOTS], logits[:], -1.0, 0.0, op0=ALU.mult, op1=ALU.min, accum_out=shift[:]
             )
+
+            weights = work.tile([P, KEYS], F32, name="weights")
+            denominator = work.tile([P, 1], F32, name="denominator")
+            nc.scalar.activation(
+                weights[:], negated[:], ACT.Exp, bias=shift[:], scale=-1.0, accum_out=denominator[:]
+            )
+
             inverse = work.tile([P, 1], F32, name="inverse")
             nc.vector.reciprocal(inverse[:], denominator[:])
-
-            nc.vector.tensor_scalar(weights[:], weights[:], inverse[:], float(SLOTS), op0=ALU.mult, op1=ALU.mult)
-            nc.sync.dma_start(out[rows, :], weights[:])
+            nc.vector.tensor_scalar(
+                weights[:, 0:SLOTS], weights[:, 0:SLOTS], inverse[:], float(SLOTS), op0=ALU.mult, op1=ALU.mult
+            )
+            nc.sync.dma_start(out[rows, :], weights[:, 0:SLOTS])

@@ -27,9 +27,11 @@ def tile_causalselfattention_kernel(tc, base, fresh, offs, out):
         for head in range(HEADS):
             rows = slice(head * P, (head + 1) * P)
             logits = work.tile([P, SLOTS], F32, name="logits")
-            nc.sync.dma_start(logits[:], base[rows, :])
+            nc.sync.dma_start(logits[:, 0 : SLOTS // 2], base[rows, 0 : SLOTS // 2])
+            nc.scalar.dma_start(logits[:, SLOTS // 2 : SLOTS], base[rows, SLOTS // 2 : SLOTS])
             retrieved = work.tile([P, N], F32, name="retrieved")
-            nc.scalar.dma_start(retrieved[:], fresh[rows, :])
+            nc.sync.dma_start(retrieved[:, 0 : N // 2], fresh[rows, 0 : N // 2])
+            nc.scalar.dma_start(retrieved[:, N // 2 : N], fresh[rows, N // 2 : N])
             logits_of.append(logits)
             retrieved_of.append(retrieved)
 
@@ -71,4 +73,5 @@ def tile_causalselfattention_kernel(tc, base, fresh, offs, out):
             nc.vector.tensor_scalar(
                 weights[:, 0:SLOTS], weights[:, 0:SLOTS], inverse[:], float(SLOTS), op0=ALU.mult, op1=ALU.mult
             )
-            nc.sync.dma_start(out[rows, :], weights[:, 0:SLOTS])
+            nc.sync.dma_start(out[rows, 0 : SLOTS // 2], weights[:, 0 : SLOTS // 2])
+            nc.scalar.dma_start(out[rows, SLOTS // 2 : SLOTS], weights[:, SLOTS // 2 : SLOTS])

@@ -19,24 +19,23 @@ def tile_causalselfattention_kernel(tc, base, fresh, offs, out):
         tc.tile_pool(name="held", bufs=1) as held,
         tc.tile_pool(name="work", bufs=HEADS) as work,
     ):
+        warm = held.tile([P, 1], F32, name="warm")
+        nc.gpsimd.memset(warm[:], 0.0)
+
         offsets = held.tile([P, N // 16], U16, name="offsets")
         nc.sync.dma_start(offsets[:], offs)
-
         logits_of = []
         retrieved_of = []
         for head in range(HEADS):
             rows = slice(head * P, (head + 1) * P)
             logits = work.tile([P, SLOTS], F32, name="logits")
-            nc.sync.dma_start(logits[:, 0 : SLOTS // 2], base[rows, 0 : SLOTS // 2])
-            nc.scalar.dma_start(logits[:, SLOTS // 2 : SLOTS], base[rows, SLOTS // 2 : SLOTS])
+            base_queue = nc.scalar if head == 0 else nc.sync
+            base_queue.dma_start(logits[:], base[rows, :])
             retrieved = work.tile([P, N], F32, name="retrieved")
-            nc.sync.dma_start(retrieved[:, 0 : N // 2], fresh[rows, 0 : N // 2])
-            nc.scalar.dma_start(retrieved[:, N // 2 : N], fresh[rows, N // 2 : N])
+            nc.sync.dma_start(retrieved[:], fresh[rows, :])
             logits_of.append(logits)
             retrieved_of.append(retrieved)
 
-        warm = held.tile([P, 1], F32, name="warm")
-        nc.vector.memset(warm[:], 0.0)
         nc.scalar.activation(warm[:], warm[:], ACT.Exp)
 
         causal = held.tile([P, P], F32, name="causal")
@@ -73,5 +72,4 @@ def tile_causalselfattention_kernel(tc, base, fresh, offs, out):
             nc.vector.tensor_scalar(
                 weights[:, 0:SLOTS], weights[:, 0:SLOTS], inverse[:], float(SLOTS), op0=ALU.mult, op1=ALU.mult
             )
-            nc.sync.dma_start(out[rows, 0 : SLOTS // 2], weights[:, 0 : SLOTS // 2])
-            nc.scalar.dma_start(out[rows, SLOTS // 2 : SLOTS], weights[:, SLOTS // 2 : SLOTS])
+            nc.sync.dma_start(out[rows, :], weights[:, 0:SLOTS])

@@ -19,23 +19,22 @@ def tile_causalselfattention_kernel(tc, base, fresh, offs, out):
         tc.tile_pool(name="held", bufs=1) as held,
         tc.tile_pool(name="work", bufs=HEADS) as work,
     ):
-        warm = held.tile([P, 1], F32, name="warm")
-        nc.gpsimd.memset(warm[:], 0.0)
-
         offsets = held.tile([P, N // 16], U16, name="offsets")
-        nc.sync.dma_start(offsets[:], offs)
         logits_of = []
         retrieved_of = []
         for head in range(HEADS):
             rows = slice(head * P, (head + 1) * P)
             logits = work.tile([P, SLOTS], F32, name="logits")
-            base_queue = nc.scalar if head == 0 else nc.sync
-            base_queue.dma_start(logits[:], base[rows, :])
+            nc.sync.dma_start(logits[:], base[rows, :])
             retrieved = work.tile([P, N], F32, name="retrieved")
-            nc.sync.dma_start(retrieved[:], fresh[rows, :])
+            nc.scalar.dma_start(retrieved[:], fresh[rows, :])
+            if head == 0:
+                nc.sync.dma_start(offsets[:], offs)
             logits_of.append(logits)
             retrieved_of.append(retrieved)
 
+        warm = held.tile([P, 1], F32, name="warm")
+        nc.vector.memset(warm[:], 0.0)
         nc.scalar.activation(warm[:], warm[:], ACT.Exp)
 
         causal = held.tile([P, P], F32, name="causal")

@@ -10,6 +10,7 @@ HEADS = 2
 SLOTS = 256
 N = 192
 KEYS = SLOTS + P
+ALIGN = 256
 MASKED = 1.0e4
 
 
@@ -24,9 +25,9 @@ def tile_causalselfattention_kernel(tc, base, fresh, offs, out):
         retrieved_of = []
         for head in range(HEADS):
             rows = slice(head * P, (head + 1) * P)
-            logits = work.tile([P, SLOTS], F32, name="logits")
+            logits = work.tile([P, SLOTS], F32, name="logits", align_bytes=ALIGN)
             nc.sync.dma_start(logits[:], base[rows, :])
-            retrieved = work.tile([P, N], F32, name="retrieved")
+            retrieved = work.tile([P, N], F32, name="retrieved", align_bytes=ALIGN)
             nc.scalar.dma_start(retrieved[:], fresh[rows, :])
             if head == 0:
                 nc.sync.dma_start(offsets[:], offs)
@@ -44,7 +45,7 @@ def tile_causalselfattention_kernel(tc, base, fresh, offs, out):
         )
         negated_of = []
         for head in range(HEADS):
-            negated = work.tile([P, KEYS], F32, name="negated")
+            negated = work.tile([P, KEYS], F32, name="negated", align_bytes=ALIGN)
             nc.gpsimd.tensor_copy(negated[:, SLOTS:KEYS], causal[:])
             negated_of.append(negated)
 
@@ -60,7 +61,7 @@ def tile_causalselfattention_kernel(tc, base, fresh, offs, out):
                 negated[:, 0:SLOTS], logits[:], -1.0, 0.0, op0=ALU.mult, op1=ALU.min, accum_out=shift[:]
             )
 
-            weights = work.tile([P, KEYS], F32, name="weights")
+            weights = work.tile([P, KEYS], F32, name="weights", align_bytes=ALIGN)
             denominator = work.tile([P, 1], F32, name="denominator")
             nc.scalar.activation(
                 weights[:], negated[:], ACT.Exp, bias=shift[:], scale=-1.0, accum_out=denominator[:]

@@ -72,4 +72,5 @@ def tile_causalselfattention_kernel(tc, base, fresh, offs, out):
             nc.vector.tensor_scalar(
                 weights[:, 0:SLOTS], weights[:, 0:SLOTS], inverse[:], float(SLOTS), op0=ALU.mult, op1=ALU.mult
             )
-            nc.sync.dma_start(out[rows, :], weights[:, 0:SLOTS])
+            store_queue = nc.sync if head == HEADS - 1 else nc.scalar
+            store_queue.dma_start(out[rows, :], weights[:, 0:SLOTS])

import concourse.mybir as mybir

F32 = mybir.dt.float32
U16 = mybir.dt.uint16
ACT = mybir.ActivationFunctionType
ALU = mybir.AluOpType

P = 128
HEADS = 2
SLOTS = 256
N = 192
KEYS = SLOTS + P
ALIGN = 256
MASKED = 1.0e4


def tile_causalselfattention_kernel(tc, base, fresh, offs, out):
    nc = tc.nc
    with (
        tc.tile_pool(name="held", bufs=1) as held,
        tc.tile_pool(name="work", bufs=HEADS) as work,
    ):
        offsets = held.tile([P, N // 16], U16, name="offsets")
        logits_of = []
        retrieved_of = []
        for head in range(HEADS):
            rows = slice(head * P, (head + 1) * P)
            logits = work.tile([P, SLOTS], F32, name="logits", align_bytes=ALIGN)
            nc.sync.dma_start(logits[:], base[rows, :])
            retrieved = work.tile([P, N], F32, name="retrieved", align_bytes=ALIGN)
            nc.scalar.dma_start(retrieved[:], fresh[rows, :])
            if head == 0:
                nc.sync.dma_start(offsets[:], offs)
            logits_of.append(logits)
            retrieved_of.append(retrieved)

        warm = held.tile([P, 1], F32, name="warm")
        nc.vector.memset(warm[:], 0.0)
        nc.scalar.activation(warm[:], warm[:], ACT.Exp)

        causal = held.tile([P, P], F32, name="causal")
        nc.gpsimd.memset(causal[:], 0.0)
        nc.gpsimd.affine_select(
            causal[:], causal[:], pattern=[[-1, P]], compare_op=ALU.is_ge, fill=MASKED, base=0, channel_multiplier=1
        )
        negated_of = []
        for head in range(HEADS):
            negated = work.tile([P, KEYS], F32, name="negated", align_bytes=ALIGN)
            nc.gpsimd.tensor_copy(negated[:, SLOTS:KEYS], causal[:])
            negated_of.append(negated)

        for head in range(HEADS):
            rows = slice(head * P, (head + 1) * P)
            logits = logits_of[head]
            negated = negated_of[head]

            nc.scalar.activation(logits[:].indirect(offsets[:]), retrieved_of[head][:], ACT.Copy)

            shift = work.tile([P, 1], F32, name="shift")
            nc.vector.tensor_scalar(
                negated[:, 0:SLOTS], logits[:], -1.0, 0.0, op0=ALU.mult, op1=ALU.min, accum_out=shift[:]
            )

            weights = work.tile([P, KEYS], F32, name="weights", align_bytes=ALIGN)
            denominator = work.tile([P, 1], F32, name="denominator")
            nc.scalar.activation(
                weights[:], negated[:], ACT.Exp, bias=shift[:], scale=-1.0, accum_out=denominator[:]
            )

            inverse = work.tile([P, 1], F32, name="inverse")
            nc.vector.reciprocal(inverse[:], denominator[:])
            nc.vector.tensor_scalar(
                weights[:, 0:SLOTS], weights[:, 0:SLOTS], inverse[:], float(SLOTS), op0=ALU.mult, op1=ALU.mult
            )
            store_queue = nc.sync if head == HEADS - 1 else nc.scalar
            store_queue.dma_start(out[rows, :], weights[:, 0:SLOTS])
